import numpy as np
import ml_dtypes


def mxq(x, axis, fmt="e4m3"):
    dtype, down = {"e4m3": (ml_dtypes.float8_e4m3fn, 7), "e5m2": (ml_dtypes.float8_e5m2, 14)}[fmt]
    v = np.moveaxis(np.asarray(x, np.float32).astype(ml_dtypes.bfloat16).astype(np.float64), axis, -1)
    blocks = v.reshape(v.shape[:-1] + (-1, 32))
    amax = np.abs(blocks).max(-1, keepdims=True)
    byte = np.maximum(np.where(amax > 0, np.frexp(amax)[1] - 1 + 127, 0) - down, 1)
    scale = np.exp2(byte - 127.0)
    codes = (blocks / scale).astype(np.float32).astype(dtype).astype(np.float64)
    return np.moveaxis((codes * scale).reshape(v.shape), -1, axis)


WIDE = False


def mx_kscale(k):
    if not WIDE:
        return np.ones(k)
    levels = np.array([10, -10, 5, -5, 0])
    if k % 512:
        return np.exp2(np.random.permutation(np.resize(levels, k // 32))).repeat(32)
    a = np.empty((k // 512, 16))
    for p in range(k // 512):
        a[p, :8] = np.random.permutation(np.resize(levels, 8))
        for g in range(8):
            far = levels[np.abs(levels - a[p, g]) >= 10]
            a[p, g + 8] = far[np.random.randint(len(far))]
    return np.exp2(a.ravel()).repeat(32)


BF16 = ml_dtypes.bfloat16


def bf(x):
    return np.asarray(x, np.float32).astype(BF16)


def f64(x):
    return np.asarray(x).astype(np.float64)


E2M1 = np.array([0.0, 0.5, 1.0, 1.5, 2.0, 3.0, 4.0, 6.0, -0.0, -0.5, -1.0, -1.5, -2.0, -3.0, -4.0, -6.0])


def pack_weight(w, fmt):
    k, n = w.shape
    w = f64(bf(w)).reshape(k // 32, 32, n)
    amax = np.abs(w).max(1)
    if fmt == "e4m3":
        byte = np.frexp(amax)[1] - 1 + 127 - 7
    else:
        mant, ex = np.frexp(amax / 6.0)
        byte = np.where(mant > 0.5, ex, ex - 1) + 127
    byte = np.clip(np.where(amax > 0, byte, 1), 1, 254)
    scaled = (w * np.exp2(127.0 - byte)[:, None, :]).reshape(k, n).astype(np.float32)
    by_word = np.ascontiguousarray(scaled.reshape(k // 512, 128, 4, n).transpose(0, 1, 3, 2))
    if fmt == "e4m3":
        words = by_word.astype(ml_dtypes.float8_e4m3fn).view(np.uint8)
    else:
        c = by_word.astype(ml_dtypes.float4_e2m1fn).view(np.uint8) & 0xF
        words = c[..., 0::2] | (c[..., 1::2] << 4)
    return np.ascontiguousarray(words), np.ascontiguousarray(byte.astype(np.uint8).reshape(k // 512, 16, n))


def unpack_weight(words, scales, fmt):
    g, p, n, _ = words.shape
    if fmt == "e4m3":
        vals = np.ascontiguousarray(words).view(ml_dtypes.float8_e4m3fn).astype(np.float64)
    else:
        nib = np.empty((g, p, n, 4), np.uint8)
        nib[..., 0::2] = words & 0xF
        nib[..., 1::2] = words >> 4
        vals = E2M1[nib]
    vals = vals * np.repeat(np.exp2(scales.astype(np.float64) - 127.0), 8, axis=1)[..., None]
    return vals.transpose(0, 1, 3, 2).reshape(g * 512, n)
def pack4(w):
    words, scales = pack_weight(w, "e2m1")
    return words.reshape(words.shape[0], 128, -1), scales


def unpack4(words, scales):
    return unpack_weight(words.reshape(words.shape[0], 128, -1, 2), scales, "e2m1")


B, D, P, C, DEPTH = 4096, 1024, 512, 128, 2
INT = (1 << DEPTH) - 1
TOT = INT + INT + 1
SIGMA = 1.0


def path_probs(th):
    prob = np.ones((1, th.shape[1]))
    probs = [prob]
    off = 0
    for d in range(DEPTH):
        n = 1 << d
        t = th[off:off + n]
        left = prob * (1.0 + t) * 0.5
        right = prob * (1.0 - t) * 0.5
        prob = np.stack([left, right], axis=1).reshape(n + n, -1)
        probs.append(prob)
        off += n
    return np.concatenate(probs, axis=0)


def draw0():
    s, t = mx_kscale(D), mx_kscale(P)
    X = bf(np.random.standard_normal((B, D)) * s)
    Z_words, Z_scales = pack4((np.random.standard_normal((P, D)) * 0.25 * P / np.sqrt(D) * t[:, None] / s).T)
    W_words, W_scales = pack4((np.random.standard_normal((C * TOT, P)) * 4.0 / np.sqrt(P) / t).T)
    V_words, V_scales = pack4((np.random.standard_normal((C * TOT, P)) * 4.0 / np.sqrt(P) / t).T)
    return {"X": X,
            "Z_words": Z_words, "Z_scales": Z_scales,
            "W_words": W_words, "W_scales": W_scales,
            "V_words": V_words, "V_scales": V_scales,
            "th": bf(np.tanh(1.5 * np.random.standard_normal((INT, B))))}


def core(X, Z_words, Z_scales, W_words, W_scales, V_words, V_scales, th):
    Xp = (unpack4(Z_words, Z_scales).T @ mxq(f64(X), 1, "e4m3").T) / P
    Xq = mxq(Xp, 0, "e4m3")
    WX = (unpack4(W_words, W_scales).T @ Xq).reshape(TOT, C, B)
    VX = (unpack4(V_words, V_scales).T @ Xq).reshape(TOT, C, B)
    probs = path_probs(f64(th))
    return np.sum(probs[:, None, :] * WX * np.tanh(SIGMA * VX), axis=0)


def e4m3fn_bytes(y):
    return np.clip(np.asarray(y, np.float64), -448.0, 448.0).astype(np.float32).astype(ml_dtypes.float8_e4m3fn).view(np.uint8)


def e4m3fn_values(b):
    return np.asarray(b, np.uint8).view(ml_dtypes.float8_e4m3fn).astype(np.float64)


def setup_inputs():
    d = draw0()
    x0 = np.asarray(d['X']).astype(np.float64)
    s = (np.max(np.abs(x0), axis=(0,), keepdims=True) / 448.0).astype(np.float32)
    out = {}
    for k, v in d.items():
        if k == 'X':
            out['X_bytes'] = e4m3fn_bytes(x0 / s.astype(np.float64))
            out['X_scale'] = s
        else:
            out[k] = v
    return out


def reference(X_bytes, X_scale, Z_words, Z_scales, W_words, W_scales, V_words, V_scales, th):
    return core(e4m3fn_values(X_bytes) * X_scale.astype(np.float64), Z_words, Z_scales, W_words, W_scales, V_words, V_scales, th)

@@ -1,0 +1,274 @@
+from contextlib import ExitStack
+
+import concourse.mybir as mybir
+from concourse.masks import make_identity
+
+B, D, P, C, NODES = 4096, 1024, 512, 128, 7
+FLOPS = 2 * B * (D * P + 2 * NODES * C * P)
+
+F32 = mybir.dt.float32
+BF16 = mybir.dt.bfloat16
+I32 = mybir.dt.int32
+U32 = mybir.dt.uint32
+U8 = mybir.dt.uint8
+FP8 = mybir.dt.float8_e4m3fn
+FP8X4 = mybir.dt.float8_e4m3fn_x4
+FP4X4 = mybir.dt.float4_e2m1fn_x4
+ACT = mybir.ActivationFunctionType
+ALU = mybir.AluOpType
+
+TILES = B // 128
+NODE_COLS = NODES * C
+BLOCKS = ((0, 512), (512, 768), (768, 896))
+
+
+def tile_bonsailayer_pa_t_w4_kernel(
+    tc, X_bytes, X_scale, Z_words, Z_scales, W_words, W_scales, V_words, V_scales, th, out
+):
+    nc = tc.nc
+    with ExitStack() as ctx:
+        const = ctx.enter_context(tc.tile_pool(name="const", bufs=1))
+        work = ctx.enter_context(tc.tile_pool(name="work", bufs=3))
+        psum = ctx.enter_context(tc.psum_pool(name="psum", bufs=1))
+        ctx.enter_context(tc.manual_schedule())
+
+        xscale = const.tile([128, D], F32)
+        nc.scalar.dma_start(out=xscale[:], in_=X_scale.rearrange("o k -> (o k)").partition_broadcast(128))
+        warm = const.tile([128, 1], F32)
+        nc.vector.memset(warm[:], 0.0)
+        warm_out = const.tile([128, 1], F32)
+        nc.scalar.activation(out=warm_out[:], in_=warm[:], func=ACT.Tanh)
+
+        thr = const.tile([128, 128], BF16)
+        nc.gpsimd.memset(thr[:], 0.0)
+        zs_raw = const.tile([128, 2, P], U8, align_bytes=64)
+        nc.vector.memset(zs_raw[:].rearrange("p g n -> p (g n)").bitcast(I32), 0)
+        vs = const.tile([128, NODE_COLS], U8, align_bytes=64)
+        nc.gpsimd.memset(vs[:].bitcast(I32), 0)
+        ws = const.tile([128, NODE_COLS], U8, align_bytes=64)
+        nc.gpsimd.memset(ws[:].bitcast(I32), 0)
+        ident_bf = const.tile([128, 128], BF16)
+        make_identity(nc, ident_bf[:])
+        ident = const.tile([128, 128], F32)
+        make_identity(nc, ident[:])
+
+        zw_raw = const.tile([128, 2, 2 * P], U8, align_bytes=64)
+        nc.sync.dma_start(out=zw_raw[:], in_=Z_words.rearrange("g p n -> p g n"))
+        xb = {}
+
+        def load_x(i, n):
+            xbytes = const.tile([128, n, D], U8, name="xbytes_%d" % i, align_bytes=64)
+            nc.sync.dma_start(
+                out=xbytes[:], in_=X_bytes[128 * i : 128 * (i + n), :].rearrange("(j p) k -> p j k", p=128)
+            )
+            for j in range(n):
+                xb[i + j] = xbytes[:, j, :]
+
+        load_x(0, 1)
+        for q in range(4):
+            nc.sync.dma_start(
+                out=zs_raw[32 * q : 32 * q + 4, :, :].bitcast(I32),
+                in_=Z_scales[:, 4 * q : 4 * q + 4, :].rearrange("g q n -> q g n").bitcast(I32),
+            )
+        load_x(1, 1)
+        nc.sync.dma_start(out=thr[0 : 3 * TILES, :], in_=th.rearrange("n (i b) -> (n i) b", b=128))
+        load_x(2, 2)
+        vw = const.tile([128, 2 * NODE_COLS], U8, align_bytes=64)
+        nc.sync.dma_start(out=vw[:], in_=V_words[0])
+        for q in range(4):
+            nc.sync.dma_start(out=vs[32 * q : 32 * q + 4, :].bitcast(I32), in_=V_scales[0, 4 * q : 4 * q + 4, :].bitcast(I32))
+        ww = const.tile([128, 2 * NODE_COLS], U8, align_bytes=64)
+        nc.sync.dma_start(out=ww[:], in_=W_words[0])
+        for q in range(4):
+            nc.sync.dma_start(out=ws[32 * q : 32 * q + 4, :].bitcast(I32), in_=W_scales[0, 4 * q : 4 * q + 4, :].bitcast(I32))
+        for i in range(4, TILES, 4):
+            load_x(i, 4)
+
+        zw = const.tile([128, 2, 2 * P], U8, align_bytes=64)
+        for g in range(2):
+            nc.vector.tensor_copy(
+                out=zw[:, g, :].rearrange("p (t m b) -> p t m b", t=4, b=2),
+                in_=zw_raw[:, g, :].rearrange("p (m t b) -> p t m b", t=4, b=2),
+            )
+        zs = const.tile([128, 2, P], U8, align_bytes=64)
+        nc.vector.tensor_copy(
+            out=zs[:].rearrange("p g (t m) -> p g t m", t=4),
+            in_=zs_raw[:].rearrange("p g (m t) -> p g t m", t=4),
+        )
+
+        th_ps = psum.tile([128, 128], BF16, tag="xt", name="th_ps")
+        nc.tensor.transpose(th_ps[:], thr[:], ident_bf[:])
+        th_t = const.tile([128, 3 * TILES], F32)
+        nc.scalar.copy(out=th_t[:], in_=th_ps[:, 0 : 3 * TILES])
+        left = const.tile([128, 3 * TILES], F32)
+        nc.gpsimd.tensor_scalar(left[:], th_t[:], 0.5, 0.5, op0=ALU.mult, op1=ALU.add)
+        right = const.tile([128, 3 * TILES], F32)
+        nc.gpsimd.tensor_scalar(right[:], th_t[:], -0.5, 0.5, op0=ALU.mult, op1=ALU.add)
+        leaf = const.tile([128, 4 * TILES], F32)
+
+        def seg(ap, k):
+            return ap[:, TILES * k : TILES * (k + 1)]
+
+        nc.gpsimd.tensor_tensor(out=seg(leaf, 0), in0=seg(left, 0), in1=seg(left, 1), op=ALU.mult)
+        nc.gpsimd.tensor_tensor(out=seg(leaf, 1), in0=seg(left, 0), in1=seg(right, 1), op=ALU.mult)
+        nc.gpsimd.tensor_tensor(out=seg(leaf, 2), in0=seg(right, 0), in1=seg(left, 2), op=ALU.mult)
+        nc.gpsimd.tensor_tensor(out=seg(leaf, 3), in0=seg(right, 0), in1=seg(right, 2), op=ALU.mult)
+
+        def prob(n, i):
+            if n < 3:
+                src = left if n == 1 else right
+                return src[:, i : i + 1]
+            return leaf[:, TILES * (n - 3) + i : TILES * (n - 3) + i + 1]
+
+        xw, xt, xg, c1, s1, y, yg, c2, s2, vx, wx, tt, tp, acc, ob = (dict() for k in range(15))
+
+        def widen(i):
+            xwide = work.tile([128, D], BF16)
+            nc.vector.tensor_tensor(out=xwide[:], in0=xb[i].bitcast(FP8), in1=xscale[:], op=ALU.mult)
+            xw[i] = xwide
+
+        def turn(i):
+            xturn = psum.tile([128, 4, 128], F32, tag="xt", name="xturn")
+            words = xw.pop(i)[:].bitcast(F32)
+            for g in range(2):
+                for u in range(2):
+                    nc.tensor.transpose(xturn[:, 2 * g + u, :], words[:, 256 * g + u : 256 * (g + 1) : 2], ident[:])
+            xt[i] = xturn
+
+        def gather(i):
+            xgrp = work.tile([128, D], BF16, align_bytes=64)
+            nc.scalar.copy(
+                out=xgrp[:].bitcast(F32).rearrange("p (g r u) -> p g r u", g=2, u=2),
+                in_=xt.pop(i)[:].rearrange("p (g u) r -> p g r u", u=2),
+            )
+            xg[i] = xgrp
+
+        def quant1(i):
+            codes1 = work.tile([128, 256], U32, align_bytes=64)
+            scales1 = work.tile([128, 256], U8, align_bytes=64)
+            nc.vector.quantize_mx(out=codes1[:].bitcast(FP8X4), scales=scales1[:], in_=xg.pop(i)[:])
+            c1[i], s1[i] = codes1, scales1
+
+        def project(i):
+            yps = psum.tile([128, 4, 128], F32)
+            codes1, scales1 = c1.pop(i), s1.pop(i)
+            for t in range(4):
+                for g in range(2):
+                    nc.tensor.matmul_mx(
+                        out=yps[:, t, :],
+                        lhsT=zw[:, g, 256 * t : 256 * (t + 1)].bitcast(FP4X4),
+                        lhsT_scale=zs[:, g, 128 * t : 128 * (t + 1)],
+                        rhs=codes1[:, 128 * g : 128 * (g + 1)].bitcast(FP8X4),
+                        rhs_scale=scales1[:, 128 * g : 128 * (g + 1)],
+                        start=(g == 0),
+                        stop=(g == 1),
+                    )
+            y[i] = yps
+
+        def regroup(i):
+            ygrp = work.tile([128, P], BF16, align_bytes=64)
+            nc.scalar.activation(
+                out=ygrp[:].rearrange("p (r t) -> p r t", t=4),
+                in_=y.pop(i)[:].rearrange("p t r -> p r t"),
+                func=ACT.Copy,
+                scale=1.0 / P,
+            )
+            yg[i] = ygrp
+
+        def quant2(i):
+            codes2 = work.tile([128, 128], U32, align_bytes=64)
+            scales2 = work.tile([128, 128], U8, align_bytes=64)
+            nc.vector.quantize_mx(out=codes2[:].bitcast(FP8X4), scales=scales2[:], in_=yg.pop(i)[:])
+            c2[i], s2[i] = codes2, scales2
+
+        def classes(i):
+            codes2, scales2 = c2.pop(i), s2.pop(i)
+
+            def product(words, scales, first, second):
+                for a, b in BLOCKS:
+                    nc.tensor.matmul_mx(
+                        out=first[:, a:b] if b <= 512 else second[:, a - 512 : b - 512],
+                        lhsT=codes2[:].bitcast(FP8X4),
+                        lhsT_scale=scales2[:],
+                        rhs=words[:, 2 * a : 2 * b].bitcast(FP4X4),
+                        rhs_scale=scales[:, a:b],
+                        start=True,
+                        stop=True,
+                    )
+
+            va = psum.tile([128, 512], F32)
+            vb = psum.tile([128, 384], F32)
+            product(vw, vs, va, vb)
+            wa = psum.tile([128, 512], F32)
+            wb = psum.tile([128, 384], F32)
+            product(ww, ws, wa, wb)
+            vx[i], wx[i] = (va, vb), (wa, wb)
+
+        def squash(i):
+            va, vb = vx.pop(i)
+            tanh = work.tile([128, NODE_COLS], F32)
+            nc.scalar.activation(out=tanh[:, 0:512], in_=va[:], func=ACT.Tanh)
+            nc.scalar.activation(out=tanh[:, 512:896], in_=vb[:], func=ACT.Tanh)
+            tt[i] = tanh
+
+        def weigh(i):
+            wa, wb = wx.pop(i)
+            tanh = tt.pop(i)
+            terms = work.tile([128, NODE_COLS], F32)
+            for n in range(NODES):
+                cols = slice(C * n, C * (n + 1))
+                w = wa[:, cols] if n < 4 else wb[:, C * (n - 4) : C * (n - 3)]
+                if n == 0:
+                    nc.vector.tensor_tensor(out=terms[:, cols], in0=w, in1=tanh[:, cols], op=ALU.mult)
+                else:
+                    nc.vector.scalar_tensor_tensor(
+                        out=terms[:, cols], in0=w, scalar=prob(n, i), in1=tanh[:, cols], op0=ALU.mult, op1=ALU.mult
+                    )
+            tp[i] = terms
+
+        groups = [(4 * k, 4) for k in range(7)] + [(28, 2), (30, 1), (31, 1)]
+        starts = {a: n for a, n in groups}
+        ends = {a + n - 1: (a, n) for a, n in groups}
+        cur = {}
+
+        def total(i):
+            if i in starts:
+                accum = psum.tile([128, 512], F32, bufs=2)
+                cur["acc"], cur["first"] = accum, i
+            terms = tp.pop(i)
+            j = i - cur["first"]
+            for n in range(NODES):
+                nc.tensor.matmul(
+                    cur["acc"][:, 128 * j : 128 * (j + 1)],
+                    lhsT=terms[:, C * n : C * (n + 1)],
+                    rhs=ident[:],
+                    start=(n == 0),
+                    stop=(n == NODES - 1),
+                    is_transpose=True,
+                )
+
+        def store(i):
+            if i not in ends:
+                return
+            a, n = ends[i]
+            score = work.tile([128, 512], F32)
+            nc.scalar.copy(out=score[:, 0 : 128 * n], in_=cur["acc"][:, 0 : 128 * n])
+            nc.sync.dma_start(out=out[:, 128 * a : 128 * (a + n)], in_=score[:, 0 : 128 * n])
+
+        def at(step, lag, stage):
+            if 0 <= step - lag < TILES:
+                stage(step - lag)
+
+        for s in range(-1, TILES + 4):
+            at(s, 2, quant2)
+            at(s, 1, quant1)
+            at(s, 0, turn)
+            at(s, 4, total)
+            at(s, 3, weigh)
+            at(s, -1, widen)
+            at(s, 0, gather)
+            at(s, 4, store)
+            at(s, 1, project)
+            at(s, 2, classes)
+            at(s, 1, regroup)
+            at(s, 2, squash)

@@ -28,7 +28,7 @@ def tile_bonsailayer_pa_t_w4_kernel(
     nc = tc.nc
     with ExitStack() as ctx:
         const = ctx.enter_context(tc.tile_pool(name="const", bufs=1))
-        work = ctx.enter_context(tc.tile_pool(name="work", bufs=3))
+        work = ctx.enter_context(tc.tile_pool(name="work", bufs=4))
         psum = ctx.enter_context(tc.psum_pool(name="psum", bufs=1))
         ctx.enter_context(tc.manual_schedule())
 
@@ -120,19 +120,34 @@ def tile_bonsailayer_pa_t_w4_kernel(
                 return src[:, i : i + 1]
             return leaf[:, TILES * (n - 3) + i : TILES * (n - 3) + i + 1]
 
-        xw, xt, xg, c1, s1, y, yg, c2, s2, vx, wx, tt, tp, acc, ob = (dict() for k in range(15))
+        xw, xp, xt, xg, c1, s1, y, yg, c2, s2, vx, wx, tt, tp = (dict() for k in range(14))
 
         def widen(i):
-            xwide = work.tile([128, D], BF16)
+            xwide = work.tile([128, D], BF16, bufs=6)
             nc.vector.tensor_tensor(out=xwide[:], in0=xb[i].bitcast(FP8), in1=xscale[:], op=ALU.mult)
             xw[i] = xwide
 
+        def permute(i):
+            if i < 4:
+                return
+            xperm = work.tile([128, 512], F32)
+            nc.scalar.copy(
+                out=xperm[:].rearrange("p (g u m) -> p g u m", g=2, u=2),
+                in_=xw.pop(i)[:].bitcast(F32).rearrange("p (g m u) -> p g u m", g=2, u=2),
+            )
+            xp[i] = xperm
+
         def turn(i):
             xturn = psum.tile([128, 4, 128], F32, tag="xt", name="xturn")
-            words = xw.pop(i)[:].bitcast(F32)
-            for g in range(2):
-                for u in range(2):
-                    nc.tensor.transpose(xturn[:, 2 * g + u, :], words[:, 256 * g + u : 256 * (g + 1) : 2], ident[:])
+            if i in xp:
+                words = xp.pop(i)
+                for c in range(4):
+                    nc.tensor.transpose(xturn[:, c, :], words[:, 128 * c : 128 * (c + 1)], ident[:])
+            else:
+                words = xw.pop(i)[:].bitcast(F32)
+                for g in range(2):
+                    for u in range(2):
+                        nc.tensor.transpose(xturn[:, 2 * g + u, :], words[:, 256 * g + u : 256 * (g + 1) : 2], ident[:])
             xt[i] = xturn
 
         def gather(i):
@@ -150,7 +165,7 @@ def tile_bonsailayer_pa_t_w4_kernel(
             c1[i], s1[i] = codes1, scales1
 
         def project(i):
-            yps = psum.tile([128, 4, 128], F32)
+            yps = psum.tile([128, 4, 128], F32, bufs=2)
             codes1, scales1 = c1.pop(i), s1.pop(i)
             for t in range(4):
                 for g in range(2):
@@ -181,59 +196,58 @@ def tile_bonsailayer_pa_t_w4_kernel(
             nc.vector.quantize_mx(out=codes2[:].bitcast(FP8X4), scales=scales2[:], in_=yg.pop(i)[:])
             c2[i], s2[i] = codes2, scales2
 
-        def classes(i):
-            codes2, scales2 = c2.pop(i), s2.pop(i)
+        def product(i, words, scales, first, second):
+            for a, b in BLOCKS:
+                nc.tensor.matmul_mx(
+                    out=first[:, a:b] if b <= 512 else second[:, a - 512 : b - 512],
+                    lhsT=c2[i][:].bitcast(FP8X4),
+                    lhsT_scale=s2[i][:],
+                    rhs=words[:, 2 * a : 2 * b].bitcast(FP4X4),
+                    rhs_scale=scales[:, a:b],
+                    start=True,
+                    stop=True,
+                )
 
-            def product(words, scales, first, second):
-                for a, b in BLOCKS:
-                    nc.tensor.matmul_mx(
-                        out=first[:, a:b] if b <= 512 else second[:, a - 512 : b - 512],
-                        lhsT=codes2[:].bitcast(FP8X4),
-                        lhsT_scale=scales2[:],
-                        rhs=words[:, 2 * a : 2 * b].bitcast(FP4X4),
-                        rhs_scale=scales[:, a:b],
-                        start=True,
-                        stop=True,
-                    )
-
+        def classes_v(i):
             va = psum.tile([128, 512], F32)
             vb = psum.tile([128, 384], F32)
-            product(vw, vs, va, vb)
+            product(i, vw, vs, va, vb)
+            vx[i] = (va, vb)
+            tanh_a = work.tile([128, 512], F32)
+            tanh_b = work.tile([128, 384], F32)
+            tt[i] = (tanh_a, tanh_b)
+
+        def classes_w(i):
             wa = psum.tile([128, 512], F32)
             wb = psum.tile([128, 384], F32)
-            product(ww, ws, wa, wb)
-            vx[i], wx[i] = (va, vb), (wa, wb)
-
-        def squash(i):
-            va, vb = vx.pop(i)
-            tanh = work.tile([128, NODE_COLS], F32)
-            nc.scalar.activation(out=tanh[:, 0:512], in_=va[:], func=ACT.Tanh)
-            nc.scalar.activation(out=tanh[:, 512:896], in_=vb[:], func=ACT.Tanh)
-            tt[i] = tanh
-
-        def weigh(i):
-            wa, wb = wx.pop(i)
-            tanh = tt.pop(i)
+            product(i, ww, ws, wa, wb)
+            wx[i] = (wa, wb)
             terms = work.tile([128, NODE_COLS], F32)
-            for n in range(NODES):
-                cols = slice(C * n, C * (n + 1))
-                w = wa[:, cols] if n < 4 else wb[:, C * (n - 4) : C * (n - 3)]
-                if n == 0:
-                    nc.vector.tensor_tensor(out=terms[:, cols], in0=w, in1=tanh[:, cols], op=ALU.mult)
-                else:
-                    nc.vector.scalar_tensor_tensor(
-                        out=terms[:, cols], in0=w, scalar=prob(n, i), in1=tanh[:, cols], op0=ALU.mult, op1=ALU.mult
-                    )
             tp[i] = terms
 
-        groups = [(4 * k, 4) for k in range(7)] + [(28, 2), (30, 1), (31, 1)]
+        def squash(i, h):
+            nc.scalar.activation(out=tt[i][h][:], in_=vx[i][h][:], func=ACT.Tanh)
+
+        def weigh(i, h):
+            for n in (range(4), range(4, NODES))[h]:
+                cols = slice(C * n, C * (n + 1))
+                part = slice(C * (n - 4 * h), C * (n - 4 * h + 1))
+                w, t = wx[i][h][:, part], tt[i][h][:, part]
+                if n == 0:
+                    nc.vector.tensor_tensor(out=tp[i][:, cols], in0=w, in1=t, op=ALU.mult)
+                else:
+                    nc.vector.scalar_tensor_tensor(
+                        out=tp[i][:, cols], in0=w, scalar=prob(n, i), in1=t, op0=ALU.mult, op1=ALU.mult
+                    )
+
+        groups = [(2 * k, 2) for k in range(15)] + [(30, 1), (31, 1)]
         starts = {a: n for a, n in groups}
         ends = {a + n - 1: (a, n) for a, n in groups}
         cur = {}
 
         def total(i):
             if i in starts:
-                accum = psum.tile([128, 512], F32, bufs=2)
+                accum = psum.tile([128, 256], F32)
                 cur["acc"], cur["first"] = accum, i
             terms = tp.pop(i)
             j = i - cur["first"]
@@ -251,24 +265,45 @@ def tile_bonsailayer_pa_t_w4_kernel(
             if i not in ends:
                 return
             a, n = ends[i]
-            score = work.tile([128, 512], F32)
-            nc.scalar.copy(out=score[:, 0 : 128 * n], in_=cur["acc"][:, 0 : 128 * n])
+            score = work.tile([128, 256], F32)
+            nc.vector.tensor_copy(out=score[:, 0 : 128 * n], in_=cur["acc"][:, 0 : 128 * n])
             nc.sync.dma_start(out=out[:, 128 * a : 128 * (a + n)], in_=score[:, 0 : 128 * n])
 
-        def at(step, lag, stage):
-            if 0 <= step - lag < TILES:
-                stage(step - lag)
+        def run(stage, i, *args):
+            if 0 <= i < TILES:
+                stage(i, *args)
 
-        for s in range(-1, TILES + 4):
-            at(s, 2, quant2)
-            at(s, 1, quant1)
-            at(s, 0, turn)
-            at(s, 4, total)
-            at(s, 3, weigh)
-            at(s, -1, widen)
-            at(s, 0, gather)
-            at(s, 4, store)
-            at(s, 1, project)
-            at(s, 2, classes)
-            at(s, 1, regroup)
-            at(s, 2, squash)
+        for k in range(-2, TILES // 2 + 3):
+            a, b, c, d, e, f = 2 * k - 1, 2 * k, 2 * k - 3, 2 * k - 2, 2 * k - 6, 2 * k - 5
+            run(turn, a)
+            run(gather, a)
+            run(total, e)
+            run(store, e)
+            run(total, f)
+            run(quant1, a)
+            run(store, f)
+            run(quant2, d)
+            run(widen, 2 * k + 3)
+            run(permute, 2 * k + 2)
+            run(turn, b)
+            run(gather, b)
+            run(quant1, b)
+            run(classes_v, c)
+            run(squash, c, 0)
+            run(squash, c, 1)
+            run(classes_w, c)
+            run(weigh, c, 0)
+            run(weigh, c, 1)
+            run(widen, 2 * k + 4)
+            run(permute, 2 * k + 3)
+            run(project, a)
+            run(regroup, a)
+            run(classes_v, d)
+            run(squash, d, 1)
+            run(squash, d, 0)
+            run(project, b)
+            run(classes_w, d)
+            run(weigh, d, 1)
+            run(quant2, a)
+            run(weigh, d, 0)
+            run(regroup, b)

@@ -120,7 +120,7 @@ def tile_bonsailayer_pa_t_w4_kernel(
                 return src[:, i : i + 1]
             return leaf[:, TILES * (n - 3) + i : TILES * (n - 3) + i + 1]
 
-        xw, xp, xt, xg, c1, s1, y, yg, c2, s2, vx, wx, tt, tp = (dict() for k in range(14))
+        xw, xp, xt, xg, c1, s1, y, yg, c2, s2, vx, wx, tt, tp, wp = (dict() for k in range(15))
 
         def widen(i):
             xwide = work.tile([128, D], BF16, bufs=6)
@@ -128,7 +128,7 @@ def tile_bonsailayer_pa_t_w4_kernel(
             xw[i] = xwide
 
         def permute(i):
-            if i < 4:
+            if not (i % 2 == 1 and i > 3):
                 return
             xperm = work.tile([128, 512], F32)
             nc.scalar.copy(
@@ -228,17 +228,39 @@ def tile_bonsailayer_pa_t_w4_kernel(
         def squash(i, h):
             nc.scalar.activation(out=tt[i][h][:], in_=vx[i][h][:], func=ACT.Tanh)
 
-        def weigh(i, h):
-            for n in (range(4), range(4, NODES))[h]:
-                cols = slice(C * n, C * (n + 1))
-                part = slice(C * (n - 4 * h), C * (n - 4 * h + 1))
-                w, t = wx[i][h][:, part], tt[i][h][:, part]
-                if n == 0:
-                    nc.vector.tensor_tensor(out=tp[i][:, cols], in0=w, in1=t, op=ALU.mult)
-                else:
-                    nc.vector.scalar_tensor_tensor(
-                        out=tp[i][:, cols], in0=w, scalar=prob(n, i), in1=t, op0=ALU.mult, op1=ALU.mult
-                    )
+        def split(i):
+            return i % 2 == 0 and i > 3
+
+        def term(i, n, w, t):
+            cols = slice(C * n, C * (n + 1))
+            if n == 0:
+                nc.vector.tensor_tensor(out=tp[i][:, cols], in0=w, in1=t, op=ALU.mult)
+            else:
+                nc.vector.scalar_tensor_tensor(
+                    out=tp[i][:, cols], in0=w, scalar=prob(n, i), in1=t, op0=ALU.mult, op1=ALU.mult
+                )
+
+        def scale_w(i):
+            if not split(i):
+                return
+            wscaled = work.tile([128, 384], F32)
+            for n in range(4, NODES):
+                part = slice(C * (n - 4), C * (n - 3))
+                nc.scalar.activation(out=wscaled[:, part], in_=wx[i][1][:, part], func=ACT.Copy, scale=prob(n, i))
+            wp[i] = wscaled
+
+        def weigh_a(i):
+            for n in range(4):
+                part = slice(C * n, C * (n + 1))
+                term(i, n, wx[i][0][:, part], tt[i][0][:, part])
+
+        def weigh_b(i):
+            if split(i):
+                nc.vector.tensor_tensor(out=tp[i][:, 512:896], in0=wp[i][:], in1=tt[i][1][:], op=ALU.mult)
+                return
+            for n in range(4, NODES):
+                part = slice(C * (n - 4), C * (n - 3))
+                term(i, n, wx[i][1][:, part], tt[i][1][:, part])
 
         groups = [(2 * k, 2) for k in range(15)] + [(30, 1), (31, 1)]
         starts = {a: n for a, n in groups}
@@ -266,44 +288,32 @@ def tile_bonsailayer_pa_t_w4_kernel(
                 return
             a, n = ends[i]
             score = work.tile([128, 256], F32)
-            nc.vector.tensor_copy(out=score[:, 0 : 128 * n], in_=cur["acc"][:, 0 : 128 * n])
+            nc.scalar.copy(out=score[:, 0 : 128 * n], in_=cur["acc"][:, 0 : 128 * n])
             nc.sync.dma_start(out=out[:, 128 * a : 128 * (a + n)], in_=score[:, 0 : 128 * n])
 
         def run(stage, i, *args):
             if 0 <= i < TILES:
                 stage(i, *args)
 
-        for k in range(-2, TILES // 2 + 3):
-            a, b, c, d, e, f = 2 * k - 1, 2 * k, 2 * k - 3, 2 * k - 2, 2 * k - 6, 2 * k - 5
-            run(turn, a)
-            run(gather, a)
-            run(total, e)
-            run(store, e)
-            run(total, f)
-            run(quant1, a)
-            run(store, f)
-            run(quant2, d)
-            run(widen, 2 * k + 3)
-            run(permute, 2 * k + 2)
-            run(turn, b)
-            run(gather, b)
-            run(quant1, b)
-            run(classes_v, c)
-            run(squash, c, 0)
-            run(squash, c, 1)
-            run(classes_w, c)
-            run(weigh, c, 0)
-            run(weigh, c, 1)
-            run(widen, 2 * k + 4)
-            run(permute, 2 * k + 3)
-            run(project, a)
-            run(regroup, a)
-            run(classes_v, d)
-            run(squash, d, 1)
-            run(squash, d, 0)
-            run(project, b)
-            run(classes_w, d)
-            run(weigh, d, 1)
-            run(quant2, a)
-            run(weigh, d, 0)
-            run(regroup, b)
+        def run(stage, i, *args):
+            if 0 <= i < TILES:
+                stage(i, *args)
+
+        for s in range(-2, TILES + 5):
+            run(turn, s)
+            run(total, s - 5)
+            run(classes_v, s - 3)
+            run(project, s - 1)
+            run(classes_w, s - 3)
+            run(permute, s + 1)
+            run(gather, s)
+            run(store, s - 5)
+            run(squash, s - 3, 0)
+            run(squash, s - 3, 1)
+            run(scale_w, s - 3)
+            run(regroup, s - 1)
+            run(widen, s + 2)
+            run(quant2, s - 2)
+            run(quant1, s)
+            run(weigh_a, s - 3)
+            run(weigh_b, s - 3)

@@ -39,21 +39,19 @@ def tile_bonsailayer_pa_t_w4_kernel(
         warm_out = const.tile([128, 1], F32)
         nc.scalar.activation(out=warm_out[:], in_=warm[:], func=ACT.Tanh)
 
-        thr = const.tile([128, 128], BF16)
-        nc.gpsimd.memset(thr[:], 0.0)
-        zs_raw = const.tile([128, 2, P], U8, align_bytes=64)
-        nc.vector.memset(zs_raw[:].rearrange("p g n -> p (g n)").bitcast(I32), 0)
-        vs = const.tile([128, NODE_COLS], U8, align_bytes=64)
-        nc.gpsimd.memset(vs[:].bitcast(I32), 0)
-        ws = const.tile([128, NODE_COLS], U8, align_bytes=64)
-        nc.gpsimd.memset(ws[:].bitcast(I32), 0)
-        ident_bf = const.tile([128, 128], BF16)
-        make_identity(nc, ident_bf[:])
         ident = const.tile([128, 128], F32)
         make_identity(nc, ident[:])
+        zs_raw = const.tile([128, 2, P], U8, align_bytes=64)
+        nc.vector.memset(zs_raw[:].bitcast(I32), 0)
+        vs = const.tile([128, NODE_COLS], U8, align_bytes=64)
+        nc.vector.memset(vs[:].bitcast(I32), 0)
+        ws = const.tile([128, NODE_COLS], U8, align_bytes=64)
+        nc.vector.memset(ws[:].bitcast(I32), 0)
+        thr = const.tile([128, 128], BF16)
+        nc.gpsimd.memset(thr[:], 0.0)
+        ident_bf = const.tile([128, 128], BF16)
+        make_identity(nc, ident_bf[:])
 
-        zw_raw = const.tile([128, 2, 2 * P], U8, align_bytes=64)
-        nc.sync.dma_start(out=zw_raw[:], in_=Z_words.rearrange("g p n -> p g n"))
         xb = {}
 
         def load_x(i, n):
@@ -64,6 +62,8 @@ def tile_bonsailayer_pa_t_w4_kernel(
             for j in range(n):
                 xb[i + j] = xbytes[:, j, :]
 
+        zw_raw = const.tile([128, 2, 2 * P], U8, align_bytes=64)
+        nc.sync.dma_start(out=zw_raw[:], in_=Z_words.rearrange("g p n -> p g n"))
         load_x(0, 1)
         for q in range(4):
             nc.sync.dma_start(
@@ -71,8 +71,8 @@ def tile_bonsailayer_pa_t_w4_kernel(
                 in_=Z_scales[:, 4 * q : 4 * q + 4, :].rearrange("g q n -> q g n").bitcast(I32),
             )
         load_x(1, 1)
-        nc.sync.dma_start(out=thr[0 : 3 * TILES, :], in_=th.rearrange("n (i b) -> (n i) b", b=128))
         load_x(2, 2)
+        nc.sync.dma_start(out=thr[0 : 3 * TILES, :], in_=th.rearrange("n (i b) -> (n i) b", b=128))
         vw = const.tile([128, 2 * NODE_COLS], U8, align_bytes=64)
         nc.sync.dma_start(out=vw[:], in_=V_words[0])
         for q in range(4):
@@ -85,34 +85,37 @@ def tile_bonsailayer_pa_t_w4_kernel(
             load_x(i, 4)
 
         zw = const.tile([128, 2, 2 * P], U8, align_bytes=64)
-        for g in range(2):
+
+        def reorder_z(g):
             nc.vector.tensor_copy(
                 out=zw[:, g, :].rearrange("p (t m b) -> p t m b", t=4, b=2),
                 in_=zw_raw[:, g, :].rearrange("p (m t b) -> p t m b", t=4, b=2),
             )
+
         zs = const.tile([128, 2, P], U8, align_bytes=64)
-        nc.vector.tensor_copy(
+        nc.gpsimd.tensor_copy(
             out=zs[:].rearrange("p g (t m) -> p g t m", t=4),
             in_=zs_raw[:].rearrange("p g (m t) -> p g t m", t=4),
         )
 
-        th_ps = psum.tile([128, 128], BF16, tag="xt", name="th_ps")
-        nc.tensor.transpose(th_ps[:], thr[:], ident_bf[:])
         th_t = const.tile([128, 3 * TILES], F32)
-        nc.scalar.copy(out=th_t[:], in_=th_ps[:, 0 : 3 * TILES])
         left = const.tile([128, 3 * TILES], F32)
-        nc.gpsimd.tensor_scalar(left[:], th_t[:], 0.5, 0.5, op0=ALU.mult, op1=ALU.add)
         right = const.tile([128, 3 * TILES], F32)
-        nc.gpsimd.tensor_scalar(right[:], th_t[:], -0.5, 0.5, op0=ALU.mult, op1=ALU.add)
         leaf = const.tile([128, 4 * TILES], F32)
 
         def seg(ap, k):
             return ap[:, TILES * k : TILES * (k + 1)]
 
-        nc.gpsimd.tensor_tensor(out=seg(leaf, 0), in0=seg(left, 0), in1=seg(left, 1), op=ALU.mult)
-        nc.gpsimd.tensor_tensor(out=seg(leaf, 1), in0=seg(left, 0), in1=seg(right, 1), op=ALU.mult)
-        nc.gpsimd.tensor_tensor(out=seg(leaf, 2), in0=seg(right, 0), in1=seg(left, 2), op=ALU.mult)
-        nc.gpsimd.tensor_tensor(out=seg(leaf, 3), in0=seg(right, 0), in1=seg(right, 2), op=ALU.mult)
+        def probabilities():
+            th_ps = psum.tile([128, 128], BF16, tag="xt", name="th_ps")
+            nc.tensor.transpose(th_ps[:], thr[:], ident_bf[:])
+            nc.scalar.copy(out=th_t[:], in_=th_ps[:, 0 : 3 * TILES])
+            nc.gpsimd.tensor_scalar(left[:], th_t[:], 0.5, 0.5, op0=ALU.mult, op1=ALU.add)
+            nc.gpsimd.tensor_scalar(right[:], th_t[:], -0.5, 0.5, op0=ALU.mult, op1=ALU.add)
+            nc.gpsimd.tensor_tensor(out=seg(leaf, 0), in0=seg(left, 0), in1=seg(left, 1), op=ALU.mult)
+            nc.gpsimd.tensor_tensor(out=seg(leaf, 1), in0=seg(left, 0), in1=seg(right, 1), op=ALU.mult)
+            nc.gpsimd.tensor_tensor(out=seg(leaf, 2), in0=seg(right, 0), in1=seg(left, 2), op=ALU.mult)
+            nc.gpsimd.tensor_tensor(out=seg(leaf, 3), in0=seg(right, 0), in1=seg(right, 2), op=ALU.mult)
 
         def prob(n, i):
             if n < 3:
@@ -120,34 +123,19 @@ def tile_bonsailayer_pa_t_w4_kernel(
                 return src[:, i : i + 1]
             return leaf[:, TILES * (n - 3) + i : TILES * (n - 3) + i + 1]
 
-        xw, xp, xt, xg, c1, s1, y, yg, c2, s2, vx, wx, tt, tp, wp = (dict() for k in range(15))
+        xw, xt, xg, c1, s1, y, yg, c2, s2, vx, wx, tt, tp, wp = (dict() for k in range(14))
 
         def widen(i):
             xwide = work.tile([128, D], BF16, bufs=6)
             nc.vector.tensor_tensor(out=xwide[:], in0=xb[i].bitcast(FP8), in1=xscale[:], op=ALU.mult)
             xw[i] = xwide
 
-        def permute(i):
-            if not (i % 2 == 1 and i > 3):
-                return
-            xperm = work.tile([128, 512], F32)
-            nc.scalar.copy(
-                out=xperm[:].rearrange("p (g u m) -> p g u m", g=2, u=2),
-                in_=xw.pop(i)[:].bitcast(F32).rearrange("p (g m u) -> p g u m", g=2, u=2),
-            )
-            xp[i] = xperm
-
         def turn(i):
             xturn = psum.tile([128, 4, 128], F32, tag="xt", name="xturn")
-            if i in xp:
-                words = xp.pop(i)
-                for c in range(4):
-                    nc.tensor.transpose(xturn[:, c, :], words[:, 128 * c : 128 * (c + 1)], ident[:])
-            else:
-                words = xw.pop(i)[:].bitcast(F32)
-                for g in range(2):
-                    for u in range(2):
-                        nc.tensor.transpose(xturn[:, 2 * g + u, :], words[:, 256 * g + u : 256 * (g + 1) : 2], ident[:])
+            words = xw.pop(i)[:].bitcast(F32)
+            for g in range(2):
+                for u in range(2):
+                    nc.tensor.transpose(xturn[:, 2 * g + u, :], words[:, 256 * g + u : 256 * (g + 1) : 2], ident[:])
             xt[i] = xturn
 
         def gather(i):
@@ -165,7 +153,7 @@ def tile_bonsailayer_pa_t_w4_kernel(
             c1[i], s1[i] = codes1, scales1
 
         def project(i):
-            yps = psum.tile([128, 4, 128], F32, bufs=2)
+            yps = psum.tile([128, 4, 128], F32)
             codes1, scales1 = c1.pop(i), s1.pop(i)
             for t in range(4):
                 for g in range(2):
@@ -229,7 +217,7 @@ def tile_bonsailayer_pa_t_w4_kernel(
             nc.scalar.activation(out=tt[i][h][:], in_=vx[i][h][:], func=ACT.Tanh)
 
         def split(i):
-            return i % 2 == 0 and i > 3
+            return i % 4 != 3
 
         def term(i, n, w, t):
             cols = slice(C * n, C * (n + 1))
@@ -269,7 +257,7 @@ def tile_bonsailayer_pa_t_w4_kernel(
 
         def total(i):
             if i in starts:
-                accum = psum.tile([128, 256], F32)
+                accum = psum.tile([128, 256], F32, bufs=2)
                 cur["acc"], cur["first"] = accum, i
             terms = tp.pop(i)
             j = i - cur["first"]
@@ -295,25 +283,25 @@ def tile_bonsailayer_pa_t_w4_kernel(
             if 0 <= i < TILES:
                 stage(i, *args)
 
-        def run(stage, i, *args):
-            if 0 <= i < TILES:
-                stage(i, *args)
-
+        reorder_z(0)
         for s in range(-2, TILES + 5):
+            if s == -1:
+                reorder_z(1)
             run(turn, s)
             run(total, s - 5)
             run(classes_v, s - 3)
             run(project, s - 1)
             run(classes_w, s - 3)
-            run(permute, s + 1)
             run(gather, s)
             run(store, s - 5)
             run(squash, s - 3, 0)
             run(squash, s - 3, 1)
-            run(scale_w, s - 3)
             run(regroup, s - 1)
-            run(widen, s + 2)
+            run(scale_w, s - 3)
             run(quant2, s - 2)
             run(quant1, s)
+            run(widen, s + 2)
             run(weigh_a, s - 3)
             run(weigh_b, s - 3)
+            if s == 1:
+                probabilities()

@@ -17,9 +17,14 @@ FP4X4 = mybir.dt.float4_e2m1fn_x4
 ACT = mybir.ActivationFunctionType
 ALU = mybir.AluOpType
 
-TILES = B // 128
+TILE = 128
+TILES = B // TILE
+PASSES = D // 512
+BANK = 512
 NODE_COLS = NODES * C
-BLOCKS = ((0, 512), (512, 768), (768, 896))
+SECOND = NODE_COLS - BANK
+CUTS = ((0, 512), (512, 768), (768, 896))
+EARLY = 2
 
 
 def tile_bonsailayer_pa_t_w4_kernel(
@@ -32,239 +37,278 @@ def tile_bonsailayer_pa_t_w4_kernel(
         psum = ctx.enter_context(tc.psum_pool(name="psum", bufs=1))
         ctx.enter_context(tc.manual_schedule())
 
-        xscale = const.tile([128, D], F32)
-        nc.scalar.dma_start(out=xscale[:], in_=X_scale.rearrange("o k -> (o k)").partition_broadcast(128))
-        warm = const.tile([128, 1], F32)
-        nc.vector.memset(warm[:], 0.0)
-        warm_out = const.tile([128, 1], F32)
-        nc.scalar.activation(out=warm_out[:], in_=warm[:], func=ACT.Tanh)
+
+        k_scale = const.tile([128, 4 * PASSES], F32)
+        nc.scalar.dma_start(
+            out=k_scale[:].rearrange("p (g t) -> p g t", t=4),
+            in_=X_scale.rearrange("o (g p t) -> p (o g) t", p=128, t=4),
+        )
+
+        th_rows = const.tile([128, TILE], BF16)
+        nc.vector.memset(th_rows[:], 0.0)
+
+        one_column = const.tile([128, 1], F32)
+        nc.vector.memset(one_column[:], 0.0)
+        one_tanh = const.tile([128, 1], F32)
+        nc.scalar.activation(out=one_tanh[:], in_=one_column[:], func=ACT.Tanh)
 
         ident = const.tile([128, 128], F32)
         make_identity(nc, ident[:])
-        zs_raw = const.tile([128, 2, P], U8, align_bytes=64)
-        nc.vector.memset(zs_raw[:].bitcast(I32), 0)
-        vs = const.tile([128, NODE_COLS], U8, align_bytes=64)
-        nc.vector.memset(vs[:].bitcast(I32), 0)
-        ws = const.tile([128, NODE_COLS], U8, align_bytes=64)
-        nc.vector.memset(ws[:].bitcast(I32), 0)
-        thr = const.tile([128, 128], BF16)
-        nc.gpsimd.memset(thr[:], 0.0)
-        ident_bf = const.tile([128, 128], BF16)
-        make_identity(nc, ident_bf[:])
+        z_scales_in = const.tile([128, PASSES, P], U8, align_bytes=64)
+        nc.vector.memset(z_scales_in[:].bitcast(I32), 0)
+        v_scales = const.tile([128, 1, NODE_COLS], U8, align_bytes=64)
+        nc.vector.memset(v_scales[:].bitcast(I32), 0)
+        w_scales = const.tile([128, 1, NODE_COLS], U8, align_bytes=64)
+        nc.vector.memset(w_scales[:].bitcast(I32), 0)
+        ident_bf16 = const.tile([128, 128], BF16)
+        make_identity(nc, ident_bf16[:])
 
-        xb = {}
+        x_codes = {}
 
         def load_x(i, n):
-            xbytes = const.tile([128, n, D], U8, name="xbytes_%d" % i, align_bytes=64)
-            nc.sync.dma_start(
-                out=xbytes[:], in_=X_bytes[128 * i : 128 * (i + n), :].rearrange("(j p) k -> p j k", p=128)
-            )
+            x_bytes = const.tile([128, n, D], U8, name="x_bytes_%d" % i, align_bytes=64)
+            rows = X_bytes[TILE * i : TILE * (i + n), :]
+            nc.sync.dma_start(out=x_bytes[:], in_=rows.rearrange("(j p) k -> p j k", p=TILE))
             for j in range(n):
-                xb[i + j] = xbytes[:, j, :]
+                x_codes[i + j] = x_bytes[:, j, :]
 
-        zw_raw = const.tile([128, 2, 2 * P], U8, align_bytes=64)
-        nc.sync.dma_start(out=zw_raw[:], in_=Z_words.rearrange("g p n -> p g n"))
-        load_x(0, 1)
-        for q in range(4):
-            nc.sync.dma_start(
-                out=zs_raw[32 * q : 32 * q + 4, :, :].bitcast(I32),
-                in_=Z_scales[:, 4 * q : 4 * q + 4, :].rearrange("g q n -> q g n").bitcast(I32),
-            )
-        load_x(1, 1)
-        load_x(2, 2)
-        nc.sync.dma_start(out=thr[0 : 3 * TILES, :], in_=th.rearrange("n (i b) -> (n i) b", b=128))
-        vw = const.tile([128, 2 * NODE_COLS], U8, align_bytes=64)
-        nc.sync.dma_start(out=vw[:], in_=V_words[0])
-        for q in range(4):
-            nc.sync.dma_start(out=vs[32 * q : 32 * q + 4, :].bitcast(I32), in_=V_scales[0, 4 * q : 4 * q + 4, :].bitcast(I32))
-        ww = const.tile([128, 2 * NODE_COLS], U8, align_bytes=64)
-        nc.sync.dma_start(out=ww[:], in_=W_words[0])
-        for q in range(4):
-            nc.sync.dma_start(out=ws[32 * q : 32 * q + 4, :].bitcast(I32), in_=W_scales[0, 4 * q : 4 * q + 4, :].bitcast(I32))
+        def load_scale_bytes(scale_tile, scales):
+            for q in range(4):
+                rows = scales[:, 4 * q : 4 * (q + 1), :].rearrange("g r n -> r g n")
+                nc.sync.dma_start(out=scale_tile[32 * q : 32 * q + 4, :, :].bitcast(I32), in_=rows.bitcast(I32))
+
+        for i in range(EARLY):
+            load_x(i, 1)
+        z_words_in = const.tile([128, PASSES, 2 * P], U8, align_bytes=64)
+        nc.sync.dma_start(out=z_words_in[:], in_=Z_words.rearrange("g p n -> p g n"))
+        load_scale_bytes(z_scales_in, Z_scales)
+        x_scale = const.tile([128, D], F32)
+        nc.sync.dma_start(out=x_scale[:], in_=X_scale.rearrange("o k -> (o k)").partition_broadcast(128))
+        load_x(EARLY, 4 - EARLY)
+        nc.scalar.dma_start(out=th_rows[0 : 3 * TILES, :], in_=th.rearrange("n (i b) -> (n i) b", b=TILE))
+        v_words = const.tile([128, 2 * NODE_COLS], U8, align_bytes=64)
+        nc.sync.dma_start(out=v_words[:], in_=V_words[0])
+        load_scale_bytes(v_scales, V_scales)
+        w_words = const.tile([128, 2 * NODE_COLS], U8, align_bytes=64)
+        nc.sync.dma_start(out=w_words[:], in_=W_words[0])
+        load_scale_bytes(w_scales, W_scales)
         for i in range(4, TILES, 4):
             load_x(i, 4)
 
-        zw = const.tile([128, 2, 2 * P], U8, align_bytes=64)
+        z_words = const.tile([128, PASSES, 2 * P], U8, align_bytes=64)
+        z_scales = const.tile([128, PASSES, P], U8, align_bytes=64)
 
-        def reorder_z(g):
-            nc.vector.tensor_copy(
-                out=zw[:, g, :].rearrange("p (t m b) -> p t m b", t=4, b=2),
-                in_=zw_raw[:, g, :].rearrange("p (m t b) -> p t m b", t=4, b=2),
+        def reorder_z():
+            for g in range(PASSES):
+                nc.vector.tensor_copy(
+                    out=z_words[:, g, :].rearrange("p (t m b) -> p t m b", t=4, b=2),
+                    in_=z_words_in[:, g, :].rearrange("p (m t b) -> p t m b", t=4, b=2),
+                )
+            nc.gpsimd.tensor_copy(
+                out=z_scales[:].rearrange("p g (t m) -> p g t m", t=4),
+                in_=z_scales_in[:].rearrange("p g (m t) -> p g t m", t=4),
             )
 
-        zs = const.tile([128, 2, P], U8, align_bytes=64)
-        nc.gpsimd.tensor_copy(
-            out=zs[:].rearrange("p g (t m) -> p g t m", t=4),
-            in_=zs_raw[:].rearrange("p g (m t) -> p g t m", t=4),
-        )
-
-        th_t = const.tile([128, 3 * TILES], F32)
+        th_turned = const.tile([128, 3 * TILES], F32)
         left = const.tile([128, 3 * TILES], F32)
         right = const.tile([128, 3 * TILES], F32)
-        leaf = const.tile([128, 4 * TILES], F32)
+        leaves = const.tile([128, 4 * TILES], F32)
 
-        def seg(ap, k):
-            return ap[:, TILES * k : TILES * (k + 1)]
+        def node_columns(values, n):
+            return values[:, TILES * n : TILES * (n + 1)]
 
-        def probabilities():
-            th_ps = psum.tile([128, 128], BF16, tag="xt", name="th_ps")
-            nc.tensor.transpose(th_ps[:], thr[:], ident_bf[:])
-            nc.scalar.copy(out=th_t[:], in_=th_ps[:, 0 : 3 * TILES])
-            nc.gpsimd.tensor_scalar(left[:], th_t[:], 0.5, 0.5, op0=ALU.mult, op1=ALU.add)
-            nc.gpsimd.tensor_scalar(right[:], th_t[:], -0.5, 0.5, op0=ALU.mult, op1=ALU.add)
-            nc.gpsimd.tensor_tensor(out=seg(leaf, 0), in0=seg(left, 0), in1=seg(left, 1), op=ALU.mult)
-            nc.gpsimd.tensor_tensor(out=seg(leaf, 1), in0=seg(left, 0), in1=seg(right, 1), op=ALU.mult)
-            nc.gpsimd.tensor_tensor(out=seg(leaf, 2), in0=seg(right, 0), in1=seg(left, 2), op=ALU.mult)
-            nc.gpsimd.tensor_tensor(out=seg(leaf, 3), in0=seg(right, 0), in1=seg(right, 2), op=ALU.mult)
+        def path_probabilities():
+            th_bank = psum.tile([128, 128], BF16, tag="xp_bank", name="th_bank")
+            nc.tensor.transpose(th_bank[:], th_rows[:], ident_bf16[:])
+            nc.scalar.copy(out=th_turned[:], in_=th_bank[:, 0 : 3 * TILES])
+            nc.gpsimd.tensor_scalar(left[:], th_turned[:], 0.5, 0.5, op0=ALU.mult, op1=ALU.add)
+            nc.gpsimd.tensor_scalar(right[:], th_turned[:], -0.5, 0.5, op0=ALU.mult, op1=ALU.add)
+            for leaf, (root_side, side, parent) in enumerate(
+                ((left, left, 1), (left, right, 1), (right, left, 2), (right, right, 2))
+            ):
+                nc.gpsimd.tensor_tensor(
+                    out=node_columns(leaves, leaf),
+                    in0=node_columns(root_side, 0),
+                    in1=node_columns(side, parent),
+                    op=ALU.mult,
+                )
 
-        def prob(n, i):
-            if n < 3:
-                src = left if n == 1 else right
-                return src[:, i : i + 1]
-            return leaf[:, TILES * (n - 3) + i : TILES * (n - 3) + i + 1]
+        def probability(n, i):
+            values, column = {1: (left, i), 2: (right, i)}.get(n, (leaves, TILES * (n - 3) + i))
+            return values[:, column : column + 1]
 
-        xw, xt, xg, c1, s1, y, yg, c2, s2, vx, wx, tt, tp, wp = (dict() for k in range(14))
+        wide, turned, grouped, x_quantised, xp_banks, xp_grouped, xp_quantised = (dict() for k in range(7))
+        v_banks, w_banks, tanhs, w_scaled, terms, sum_banks = (dict() for k in range(6))
 
         def widen(i):
-            xwide = work.tile([128, D], BF16, bufs=6)
-            nc.vector.tensor_tensor(out=xwide[:], in0=xb[i].bitcast(FP8), in1=xscale[:], op=ALU.mult)
-            xw[i] = xwide
+            x_wide = work.tile([128, D], BF16, bufs=6)
+            if i == 0:
+                nc.vector.tensor_copy(out=x_wide[:], in_=x_codes[i].bitcast(FP8))
+            elif i < EARLY:
+                nc.scalar.copy(out=x_wide[:], in_=x_codes[i].bitcast(FP8))
+            else:
+                nc.vector.tensor_tensor(out=x_wide[:], in0=x_codes[i].bitcast(FP8), in1=x_scale[:], op=ALU.mult)
+            wide[i] = x_wide
 
         def turn(i):
-            xturn = psum.tile([128, 4, 128], F32, tag="xt", name="xturn")
-            words = xw.pop(i)[:].bitcast(F32)
-            for g in range(2):
+            x_bank = psum.tile([128, 2 * PASSES, TILE], F32)
+            words = wide.pop(i)[:].bitcast(F32)
+            for g in range(PASSES):
                 for u in range(2):
-                    nc.tensor.transpose(xturn[:, 2 * g + u, :], words[:, 256 * g + u : 256 * (g + 1) : 2], ident[:])
-            xt[i] = xturn
+                    nc.tensor.transpose(x_bank[:, 2 * g + u, :], words[:, 256 * g + u : 256 * (g + 1) : 2], ident[:])
+            turned[i] = x_bank
 
         def gather(i):
-            xgrp = work.tile([128, D], BF16, align_bytes=64)
-            nc.scalar.copy(
-                out=xgrp[:].bitcast(F32).rearrange("p (g r u) -> p g r u", g=2, u=2),
-                in_=xt.pop(i)[:].rearrange("p (g u) r -> p g r u", u=2),
-            )
-            xg[i] = xgrp
+            x_grouped = work.tile([128, D], BF16, align_bytes=64)
+            x_bank = turned.pop(i)
+            if i < EARLY:
+                pairs = x_bank[:].bitcast(BF16).rearrange("p (g u) (r e) -> p g r u e", u=2, e=2)
+                for g in range(PASSES):
+                    scales = k_scale[:, 4 * g : 4 * (g + 1)].rearrange("p (r u e) -> p r u e", r=1, u=2)
+                    nc.vector.tensor_tensor(
+                        out=x_grouped[:, 512 * g : 512 * (g + 1)].rearrange("p (r u e) -> p r u e", u=2, e=2),
+                        in0=pairs[:, g],
+                        in1=scales.to_broadcast([128, TILE, 2, 2]),
+                        op=ALU.mult,
+                    )
+            else:
+                nc.scalar.copy(
+                    out=x_grouped[:].bitcast(F32).rearrange("p (g r u) -> p g r u", g=PASSES, u=2),
+                    in_=x_bank[:].rearrange("p (g u) r -> p g r u", u=2),
+                )
+            grouped[i] = x_grouped
 
-        def quant1(i):
-            codes1 = work.tile([128, 256], U32, align_bytes=64)
-            scales1 = work.tile([128, 256], U8, align_bytes=64)
-            nc.vector.quantize_mx(out=codes1[:].bitcast(FP8X4), scales=scales1[:], in_=xg.pop(i)[:])
-            c1[i], s1[i] = codes1, scales1
+        def quantise_x(i):
+            x_words = work.tile([128, PASSES * TILE], U32, align_bytes=64)
+            x_word_scales = work.tile([128, PASSES * TILE], U8, align_bytes=64)
+            nc.vector.quantize_mx(out=x_words[:].bitcast(FP8X4), scales=x_word_scales[:], in_=grouped.pop(i)[:])
+            x_quantised[i] = (x_words, x_word_scales)
 
         def project(i):
-            yps = psum.tile([128, 4, 128], F32)
-            codes1, scales1 = c1.pop(i), s1.pop(i)
+            xp_bank = psum.tile([128, 4, TILE], F32)
+            x_words, x_word_scales = x_quantised.pop(i)
             for t in range(4):
-                for g in range(2):
+                for g in range(PASSES):
+                    samples = slice(TILE * g, TILE * (g + 1))
                     nc.tensor.matmul_mx(
-                        out=yps[:, t, :],
-                        lhsT=zw[:, g, 256 * t : 256 * (t + 1)].bitcast(FP4X4),
-                        lhsT_scale=zs[:, g, 128 * t : 128 * (t + 1)],
-                        rhs=codes1[:, 128 * g : 128 * (g + 1)].bitcast(FP8X4),
-                        rhs_scale=scales1[:, 128 * g : 128 * (g + 1)],
+                        out=xp_bank[:, t, :],
+                        lhsT=z_words[:, g, 256 * t : 256 * (t + 1)].bitcast(FP4X4),
+                        lhsT_scale=z_scales[:, g, 128 * t : 128 * (t + 1)],
+                        rhs=x_words[:, samples].bitcast(FP8X4),
+                        rhs_scale=x_word_scales[:, samples],
                         start=(g == 0),
-                        stop=(g == 1),
+                        stop=(g == PASSES - 1),
                     )
-            y[i] = yps
+            xp_banks[i] = xp_bank
 
         def regroup(i):
-            ygrp = work.tile([128, P], BF16, align_bytes=64)
+            xp_group = work.tile([128, P], BF16, align_bytes=64)
             nc.scalar.activation(
-                out=ygrp[:].rearrange("p (r t) -> p r t", t=4),
-                in_=y.pop(i)[:].rearrange("p t r -> p r t"),
+                out=xp_group[:].rearrange("p (r t) -> p r t", t=4),
+                in_=xp_banks.pop(i)[:].rearrange("p t r -> p r t"),
                 func=ACT.Copy,
                 scale=1.0 / P,
             )
-            yg[i] = ygrp
+            xp_grouped[i] = xp_group
 
-        def quant2(i):
-            codes2 = work.tile([128, 128], U32, align_bytes=64)
-            scales2 = work.tile([128, 128], U8, align_bytes=64)
-            nc.vector.quantize_mx(out=codes2[:].bitcast(FP8X4), scales=scales2[:], in_=yg.pop(i)[:])
-            c2[i], s2[i] = codes2, scales2
+        def quantise_xp(i):
+            xp_words = work.tile([128, TILE], U32, align_bytes=64)
+            xp_word_scales = work.tile([128, TILE], U8, align_bytes=64)
+            nc.vector.quantize_mx(out=xp_words[:].bitcast(FP8X4), scales=xp_word_scales[:], in_=xp_grouped.pop(i)[:])
+            xp_quantised[i] = (xp_words, xp_word_scales)
 
-        def product(i, words, scales, first, second):
-            for a, b in BLOCKS:
+        def class_products(i, words, scales, banks):
+            xp_words, xp_word_scales = xp_quantised[i]
+            for a, b in CUTS:
                 nc.tensor.matmul_mx(
-                    out=first[:, a:b] if b <= 512 else second[:, a - 512 : b - 512],
-                    lhsT=c2[i][:].bitcast(FP8X4),
-                    lhsT_scale=s2[i][:],
+                    out=banks[0][:, a:b] if b <= BANK else banks[1][:, a - BANK : b - BANK],
+                    lhsT=xp_words[:].bitcast(FP8X4),
+                    lhsT_scale=xp_word_scales[:],
                     rhs=words[:, 2 * a : 2 * b].bitcast(FP4X4),
-                    rhs_scale=scales[:, a:b],
+                    rhs_scale=scales[:, 0, a:b],
                     start=True,
                     stop=True,
                 )
 
         def classes_v(i):
-            va = psum.tile([128, 512], F32)
-            vb = psum.tile([128, 384], F32)
-            product(i, vw, vs, va, vb)
-            vx[i] = (va, vb)
-            tanh_a = work.tile([128, 512], F32)
-            tanh_b = work.tile([128, 384], F32)
-            tt[i] = (tanh_a, tanh_b)
+            v_first = psum.tile([128, BANK], F32)
+            v_second = psum.tile([128, SECOND], F32)
+            v_banks[i] = (v_first, v_second)
+            class_products(i, v_words, v_scales, v_banks[i])
 
         def classes_w(i):
-            wa = psum.tile([128, 512], F32)
-            wb = psum.tile([128, 384], F32)
-            product(i, ww, ws, wa, wb)
-            wx[i] = (wa, wb)
-            terms = work.tile([128, NODE_COLS], F32)
-            tp[i] = terms
+            w_first = psum.tile([128, BANK], F32)
+            w_second = psum.tile([128, SECOND], F32)
+            w_banks[i] = (w_first, w_second)
+            class_products(i, w_words, w_scales, w_banks[i])
+            node_terms = work.tile([128, NODE_COLS], F32)
+            terms[i] = node_terms
 
-        def squash(i, h):
-            nc.scalar.activation(out=tt[i][h][:], in_=vx[i][h][:], func=ACT.Tanh)
+        def squash_a(i):
+            tanh_first = work.tile([128, BANK], F32)
+            nc.scalar.activation(out=tanh_first[:], in_=v_banks[i][0][:], func=ACT.Tanh)
+            tanhs[i] = [tanh_first]
 
-        def split(i):
+        def squash_b(i):
+            tanh_second = work.tile([128, SECOND], F32)
+            nc.scalar.activation(out=tanh_second[:], in_=v_banks[i][1][:], func=ACT.Tanh)
+            tanhs[i].append(tanh_second)
+
+        def scalar_scales(i):
             return i % 4 != 3
 
-        def term(i, n, w, t):
-            cols = slice(C * n, C * (n + 1))
+        def scale_w(i):
+            if scalar_scales(i):
+                w_second_scaled = work.tile([128, SECOND], F32)
+                for n in range(4, NODES):
+                    columns = slice(C * n - BANK, C * (n + 1) - BANK)
+                    nc.scalar.activation(
+                        out=w_second_scaled[:, columns],
+                        in_=w_banks[i][1][:, columns],
+                        func=ACT.Copy,
+                        scale=probability(n, i),
+                    )
+                w_scaled[i] = w_second_scaled
+
+        def node_term(i, n):
+            half = n // 4
+            columns = slice(C * n - BANK * half, C * (n + 1) - BANK * half)
+            w, tanh = w_banks[i][half][:, columns], tanhs[i][half][:, columns]
+            term = terms[i][:, C * n : C * (n + 1)]
             if n == 0:
-                nc.vector.tensor_tensor(out=tp[i][:, cols], in0=w, in1=t, op=ALU.mult)
+                nc.vector.tensor_tensor(out=term, in0=w, in1=tanh, op=ALU.mult)
             else:
                 nc.vector.scalar_tensor_tensor(
-                    out=tp[i][:, cols], in0=w, scalar=prob(n, i), in1=t, op0=ALU.mult, op1=ALU.mult
+                    out=term, in0=w, scalar=probability(n, i), in1=tanh, op0=ALU.mult, op1=ALU.mult
                 )
-
-        def scale_w(i):
-            if not split(i):
-                return
-            wscaled = work.tile([128, 384], F32)
-            for n in range(4, NODES):
-                part = slice(C * (n - 4), C * (n - 3))
-                nc.scalar.activation(out=wscaled[:, part], in_=wx[i][1][:, part], func=ACT.Copy, scale=prob(n, i))
-            wp[i] = wscaled
 
         def weigh_a(i):
             for n in range(4):
-                part = slice(C * n, C * (n + 1))
-                term(i, n, wx[i][0][:, part], tt[i][0][:, part])
+                node_term(i, n)
 
         def weigh_b(i):
-            if split(i):
-                nc.vector.tensor_tensor(out=tp[i][:, 512:896], in0=wp[i][:], in1=tt[i][1][:], op=ALU.mult)
-                return
-            for n in range(4, NODES):
-                part = slice(C * (n - 4), C * (n - 3))
-                term(i, n, wx[i][1][:, part], tt[i][1][:, part])
+            if scalar_scales(i):
+                nc.vector.tensor_tensor(
+                    out=terms[i][:, BANK:NODE_COLS], in0=w_scaled[i][:], in1=tanhs[i][1][:], op=ALU.mult
+                )
+            else:
+                for n in range(4, NODES):
+                    node_term(i, n)
 
-        groups = [(2 * k, 2) for k in range(15)] + [(30, 1), (31, 1)]
-        starts = {a: n for a, n in groups}
-        ends = {a + n - 1: (a, n) for a, n in groups}
-        cur = {}
+        def stands_alone(i):
+            return i >= TILES - 2
 
         def total(i):
-            if i in starts:
-                accum = psum.tile([128, 256], F32, bufs=2)
-                cur["acc"], cur["first"] = accum, i
-            terms = tp.pop(i)
-            j = i - cur["first"]
+            if stands_alone(i) or i % 2 == 0:
+                sum_bank = psum.tile([128, 2 * TILE], F32, bufs=2)
+                sum_banks[i] = (sum_bank, 0)
+            else:
+                sum_banks[i] = (sum_banks[i - 1][0], TILE)
+            bank, first = sum_banks[i]
             for n in range(NODES):
                 nc.tensor.matmul(
-                    cur["acc"][:, 128 * j : 128 * (j + 1)],
-                    lhsT=terms[:, C * n : C * (n + 1)],
+                    bank[:, first : first + TILE],
+                    lhsT=terms[i][:, C * n : C * (n + 1)],
                     rhs=ident[:],
                     start=(n == 0),
                     stop=(n == NODES - 1),
@@ -272,36 +316,36 @@ def tile_bonsailayer_pa_t_w4_kernel(
                 )
 
         def store(i):
-            if i not in ends:
-                return
-            a, n = ends[i]
-            score = work.tile([128, 256], F32)
-            nc.scalar.copy(out=score[:, 0 : 128 * n], in_=cur["acc"][:, 0 : 128 * n])
-            nc.sync.dma_start(out=out[:, 128 * a : 128 * (a + n)], in_=score[:, 0 : 128 * n])
+            if stands_alone(i) or i % 2 == 1:
+                bank, first = sum_banks[i]
+                width = first + TILE
+                score = work.tile([128, 2 * TILE], F32)
+                nc.scalar.copy(out=score[:, 0:width], in_=bank[:, 0:width])
+                nc.sync.dma_start(out=out[:, TILE * (i + 1) - width : TILE * (i + 1)], in_=score[:, 0:width])
 
-        def run(stage, i, *args):
-            if 0 <= i < TILES:
-                stage(i, *args)
-
-        reorder_z(0)
-        for s in range(-2, TILES + 5):
-            if s == -1:
-                reorder_z(1)
-            run(turn, s)
-            run(total, s - 5)
-            run(classes_v, s - 3)
-            run(project, s - 1)
-            run(classes_w, s - 3)
-            run(gather, s)
-            run(store, s - 5)
-            run(squash, s - 3, 0)
-            run(squash, s - 3, 1)
-            run(regroup, s - 1)
-            run(scale_w, s - 3)
-            run(quant2, s - 2)
-            run(quant1, s)
-            run(widen, s + 2)
-            run(weigh_a, s - 3)
-            run(weigh_b, s - 3)
-            if s == 1:
-                probabilities()
+        pipeline = (
+            (turn, 0),
+            (total, 5),
+            (classes_v, 3),
+            (project, 1),
+            (classes_w, 3),
+            (gather, 0),
+            (store, 5),
+            (squash_a, 3),
+            (squash_b, 3),
+            (regroup, 1),
+            (scale_w, 3),
+            (quantise_xp, 2),
+            (quantise_x, 0),
+            (widen, -2),
+            (weigh_a, 3),
+            (weigh_b, 3),
+        )
+        once = {-2: reorder_z, 0: path_probabilities}
+        lags = [lag for stage, lag in pipeline]
+        for s in range(min(lags), TILES + max(lags)):
+            for stage, lag in pipeline:
+                if 0 <= s - lag < TILES:
+                    stage(s - lag)
+            if s in once:
+                once[s]()

from contextlib import ExitStack

import concourse.mybir as mybir
from concourse.masks import make_identity

B, D, P, C, NODES = 4096, 1024, 512, 128, 7
FLOPS = 2 * B * (D * P + 2 * NODES * C * P)

F32 = mybir.dt.float32
BF16 = mybir.dt.bfloat16
I32 = mybir.dt.int32
U32 = mybir.dt.uint32
U8 = mybir.dt.uint8
FP8 = mybir.dt.float8_e4m3fn
FP8X4 = mybir.dt.float8_e4m3fn_x4
FP4X4 = mybir.dt.float4_e2m1fn_x4
ACT = mybir.ActivationFunctionType
ALU = mybir.AluOpType

TILE = 128
TILES = B // TILE
PASSES = D // 512
BANK = 512
NODE_COLS = NODES * C
SECOND = NODE_COLS - BANK
CUTS = ((0, 512), (512, 768), (768, 896))
EARLY = 2


def tile_bonsailayer_pa_t_w4_kernel(
    tc, X_bytes, X_scale, Z_words, Z_scales, W_words, W_scales, V_words, V_scales, th, out
):
    nc = tc.nc
    with ExitStack() as ctx:
        const = ctx.enter_context(tc.tile_pool(name="const", bufs=1))
        work = ctx.enter_context(tc.tile_pool(name="work", bufs=4))
        psum = ctx.enter_context(tc.psum_pool(name="psum", bufs=1))
        ctx.enter_context(tc.manual_schedule())


        k_scale = const.tile([128, 4 * PASSES], F32)
        nc.scalar.dma_start(
            out=k_scale[:].rearrange("p (g t) -> p g t", t=4),
            in_=X_scale.rearrange("o (g p t) -> p (o g) t", p=128, t=4),
        )

        th_rows = const.tile([128, TILE], BF16)
        nc.vector.memset(th_rows[:], 0.0)

        one_column = const.tile([128, 1], F32)
        nc.vector.memset(one_column[:], 0.0)
        one_tanh = const.tile([128, 1], F32)
        nc.scalar.activation(out=one_tanh[:], in_=one_column[:], func=ACT.Tanh)

        ident = const.tile([128, 128], F32)
        make_identity(nc, ident[:])
        z_scales_in = const.tile([128, PASSES, P], U8, align_bytes=64)
        nc.vector.memset(z_scales_in[:].bitcast(I32), 0)
        v_scales = const.tile([128, 1, NODE_COLS], U8, align_bytes=64)
        nc.vector.memset(v_scales[:].bitcast(I32), 0)
        w_scales = const.tile([128, 1, NODE_COLS], U8, align_bytes=64)
        nc.vector.memset(w_scales[:].bitcast(I32), 0)
        ident_bf16 = const.tile([128, 128], BF16)
        make_identity(nc, ident_bf16[:])

        x_codes = {}

        def load_x(i, n):
            x_bytes = const.tile([128, n, D], U8, name="x_bytes_%d" % i, align_bytes=64)
            rows = X_bytes[TILE * i : TILE * (i + n), :]
            nc.sync.dma_start(out=x_bytes[:], in_=rows.rearrange("(j p) k -> p j k", p=TILE))
            for j in range(n):
                x_codes[i + j] = x_bytes[:, j, :]

        def load_scale_bytes(scale_tile, scales):
            for q in range(4):
                rows = scales[:, 4 * q : 4 * (q + 1), :].rearrange("g r n -> r g n")
                nc.sync.dma_start(out=scale_tile[32 * q : 32 * q + 4, :, :].bitcast(I32), in_=rows.bitcast(I32))

        for i in range(EARLY):
            load_x(i, 1)
        z_words_in = const.tile([128, PASSES, 2 * P], U8, align_bytes=64)
        nc.sync.dma_start(out=z_words_in[:], in_=Z_words.rearrange("g p n -> p g n"))
        load_scale_bytes(z_scales_in, Z_scales)
        x_scale = const.tile([128, D], F32)
        nc.sync.dma_start(out=x_scale[:], in_=X_scale.rearrange("o k -> (o k)").partition_broadcast(128))
        load_x(EARLY, 4 - EARLY)
        nc.scalar.dma_start(out=th_rows[0 : 3 * TILES, :], in_=th.rearrange("n (i b) -> (n i) b", b=TILE))
        v_words = const.tile([128, 2 * NODE_COLS], U8, align_bytes=64)
        nc.sync.dma_start(out=v_words[:], in_=V_words[0])
        load_scale_bytes(v_scales, V_scales)
        w_words = const.tile([128, 2 * NODE_COLS], U8, align_bytes=64)
        nc.sync.dma_start(out=w_words[:], in_=W_words[0])
        load_scale_bytes(w_scales, W_scales)
        for i in range(4, TILES, 4):
            load_x(i, 4)

        z_words = const.tile([128, PASSES, 2 * P], U8, align_bytes=64)
        z_scales = const.tile([128, PASSES, P], U8, align_bytes=64)

        def reorder_z():
            for g in range(PASSES):
                nc.vector.tensor_copy(
                    out=z_words[:, g, :].rearrange("p (t m b) -> p t m b", t=4, b=2),
                    in_=z_words_in[:, g, :].rearrange("p (m t b) -> p t m b", t=4, b=2),
                )
            nc.gpsimd.tensor_copy(
                out=z_scales[:].rearrange("p g (t m) -> p g t m", t=4),
                in_=z_scales_in[:].rearrange("p g (m t) -> p g t m", t=4),
            )

        th_turned = const.tile([128, 3 * TILES], F32)
        left = const.tile([128, 3 * TILES], F32)
        right = const.tile([128, 3 * TILES], F32)
        leaves = const.tile([128, 4 * TILES], F32)

        def node_columns(values, n):
            return values[:, TILES * n : TILES * (n + 1)]

        def path_probabilities():
            th_bank = psum.tile([128, 128], BF16, tag="xp_bank", name="th_bank")
            nc.tensor.transpose(th_bank[:], th_rows[:], ident_bf16[:])
            nc.scalar.copy(out=th_turned[:], in_=th_bank[:, 0 : 3 * TILES])
            nc.gpsimd.tensor_scalar(left[:], th_turned[:], 0.5, 0.5, op0=ALU.mult, op1=ALU.add)
            nc.gpsimd.tensor_scalar(right[:], th_turned[:], -0.5, 0.5, op0=ALU.mult, op1=ALU.add)
            for leaf, (root_side, side, parent) in enumerate(
                ((left, left, 1), (left, right, 1), (right, left, 2), (right, right, 2))
            ):
                nc.gpsimd.tensor_tensor(
                    out=node_columns(leaves, leaf),
                    in0=node_columns(root_side, 0),
                    in1=node_columns(side, parent),
                    op=ALU.mult,
                )

        def probability(n, i):
            values, column = {1: (left, i), 2: (right, i)}.get(n, (leaves, TILES * (n - 3) + i))
            return values[:, column : column + 1]

        wide, turned, grouped, x_quantised, xp_banks, xp_grouped, xp_quantised = (dict() for k in range(7))
        v_banks, w_banks, tanhs, w_scaled, terms, sum_banks = (dict() for k in range(6))

        def widen(i):
            x_wide = work.tile([128, D], BF16, bufs=6)
            if i == 0:
                nc.vector.tensor_copy(out=x_wide[:], in_=x_codes[i].bitcast(FP8))
            elif i < EARLY:
                nc.scalar.copy(out=x_wide[:], in_=x_codes[i].bitcast(FP8))
            else:
                nc.vector.tensor_tensor(out=x_wide[:], in0=x_codes[i].bitcast(FP8), in1=x_scale[:], op=ALU.mult)
            wide[i] = x_wide

        def turn(i):
            x_bank = psum.tile([128, 2 * PASSES, TILE], F32)
            words = wide.pop(i)[:].bitcast(F32)
            for g in range(PASSES):
                for u in range(2):
                    nc.tensor.transpose(x_bank[:, 2 * g + u, :], words[:, 256 * g + u : 256 * (g + 1) : 2], ident[:])
            turned[i] = x_bank

        def gather(i):
            x_grouped = work.tile([128, D], BF16, align_bytes=64)
            x_bank = turned.pop(i)
            if i < EARLY:
                pairs = x_bank[:].bitcast(BF16).rearrange("p (g u) (r e) -> p g r u e", u=2, e=2)
                for g in range(PASSES):
                    scales = k_scale[:, 4 * g : 4 * (g + 1)].rearrange("p (r u e) -> p r u e", r=1, u=2)
                    nc.vector.tensor_tensor(
                        out=x_grouped[:, 512 * g : 512 * (g + 1)].rearrange("p (r u e) -> p r u e", u=2, e=2),
                        in0=pairs[:, g],
                        in1=scales.to_broadcast([128, TILE, 2, 2]),
                        op=ALU.mult,
                    )
            else:
                nc.scalar.copy(
                    out=x_grouped[:].bitcast(F32).rearrange("p (g r u) -> p g r u", g=PASSES, u=2),
                    in_=x_bank[:].rearrange("p (g u) r -> p g r u", u=2),
                )
            grouped[i] = x_grouped

        def quantise_x(i):
            x_words = work.tile([128, PASSES * TILE], U32, align_bytes=64)
            x_word_scales = work.tile([128, PASSES * TILE], U8, align_bytes=64)
            nc.vector.quantize_mx(out=x_words[:].bitcast(FP8X4), scales=x_word_scales[:], in_=grouped.pop(i)[:])
            x_quantised[i] = (x_words, x_word_scales)

        def project(i):
            xp_bank = psum.tile([128, 4, TILE], F32)
            x_words, x_word_scales = x_quantised.pop(i)
            for t in range(4):
                for g in range(PASSES):
                    samples = slice(TILE * g, TILE * (g + 1))
                    nc.tensor.matmul_mx(
                        out=xp_bank[:, t, :],
                        lhsT=z_words[:, g, 256 * t : 256 * (t + 1)].bitcast(FP4X4),
                        lhsT_scale=z_scales[:, g, 128 * t : 128 * (t + 1)],
                        rhs=x_words[:, samples].bitcast(FP8X4),
                        rhs_scale=x_word_scales[:, samples],
                        start=(g == 0),
                        stop=(g == PASSES - 1),
                    )
            xp_banks[i] = xp_bank

        def regroup(i):
            xp_group = work.tile([128, P], BF16, align_bytes=64)
            nc.scalar.activation(
                out=xp_group[:].rearrange("p (r t) -> p r t", t=4),
                in_=xp_banks.pop(i)[:].rearrange("p t r -> p r t"),
                func=ACT.Copy,
                scale=1.0 / P,
            )
            xp_grouped[i] = xp_group

        def quantise_xp(i):
            xp_words = work.tile([128, TILE], U32, align_bytes=64)
            xp_word_scales = work.tile([128, TILE], U8, align_bytes=64)
            nc.vector.quantize_mx(out=xp_words[:].bitcast(FP8X4), scales=xp_word_scales[:], in_=xp_grouped.pop(i)[:])
            xp_quantised[i] = (xp_words, xp_word_scales)

        def class_products(i, words, scales, banks):
            xp_words, xp_word_scales = xp_quantised[i]
            for a, b in CUTS:
                nc.tensor.matmul_mx(
                    out=banks[0][:, a:b] if b <= BANK else banks[1][:, a - BANK : b - BANK],
                    lhsT=xp_words[:].bitcast(FP8X4),
                    lhsT_scale=xp_word_scales[:],
                    rhs=words[:, 2 * a : 2 * b].bitcast(FP4X4),
                    rhs_scale=scales[:, 0, a:b],
                    start=True,
                    stop=True,
                )

        def classes_v(i):
            v_first = psum.tile([128, BANK], F32)
            v_second = psum.tile([128, SECOND], F32)
            v_banks[i] = (v_first, v_second)
            class_products(i, v_words, v_scales, v_banks[i])

        def classes_w(i):
            w_first = psum.tile([128, BANK], F32)
            w_second = psum.tile([128, SECOND], F32)
            w_banks[i] = (w_first, w_second)
            class_products(i, w_words, w_scales, w_banks[i])
            node_terms = work.tile([128, NODE_COLS], F32)
            terms[i] = node_terms

        def squash_a(i):
            tanh_first = work.tile([128, BANK], F32)
            nc.scalar.activation(out=tanh_first[:], in_=v_banks[i][0][:], func=ACT.Tanh)
            tanhs[i] = [tanh_first]

        def squash_b(i):
            tanh_second = work.tile([128, SECOND], F32)
            nc.scalar.activation(out=tanh_second[:], in_=v_banks[i][1][:], func=ACT.Tanh)
            tanhs[i].append(tanh_second)

        def scalar_scales(i):
            return i % 4 != 3

        def scale_w(i):
            if scalar_scales(i):
                w_second_scaled = work.tile([128, SECOND], F32)
                for n in range(4, NODES):
                    columns = slice(C * n - BANK, C * (n + 1) - BANK)
                    nc.scalar.activation(
                        out=w_second_scaled[:, columns],
                        in_=w_banks[i][1][:, columns],
                        func=ACT.Copy,
                        scale=probability(n, i),
                    )
                w_scaled[i] = w_second_scaled

        def node_term(i, n):
            half = n // 4
            columns = slice(C * n - BANK * half, C * (n + 1) - BANK * half)
            w, tanh = w_banks[i][half][:, columns], tanhs[i][half][:, columns]
            term = terms[i][:, C * n : C * (n + 1)]
            if n == 0:
                nc.vector.tensor_tensor(out=term, in0=w, in1=tanh, op=ALU.mult)
            else:
                nc.vector.scalar_tensor_tensor(
                    out=term, in0=w, scalar=probability(n, i), in1=tanh, op0=ALU.mult, op1=ALU.mult
                )

        def weigh_a(i):
            for n in range(4):
                node_term(i, n)

        def weigh_b(i):
            if scalar_scales(i):
                nc.vector.tensor_tensor(
                    out=terms[i][:, BANK:NODE_COLS], in0=w_scaled[i][:], in1=tanhs[i][1][:], op=ALU.mult
                )
            else:
                for n in range(4, NODES):
                    node_term(i, n)

        def stands_alone(i):
            return i >= TILES - 2

        def total(i):
            if stands_alone(i) or i % 2 == 0:
                sum_bank = psum.tile([128, 2 * TILE], F32, bufs=2)
                sum_banks[i] = (sum_bank, 0)
            else:
                sum_banks[i] = (sum_banks[i - 1][0], TILE)
            bank, first = sum_banks[i]
            for n in range(NODES):
                nc.tensor.matmul(
                    bank[:, first : first + TILE],
                    lhsT=terms[i][:, C * n : C * (n + 1)],
                    rhs=ident[:],
                    start=(n == 0),
                    stop=(n == NODES - 1),
                    is_transpose=True,
                )

        def store(i):
            if stands_alone(i) or i % 2 == 1:
                bank, first = sum_banks[i]
                width = first + TILE
                score = work.tile([128, 2 * TILE], F32)
                nc.scalar.copy(out=score[:, 0:width], in_=bank[:, 0:width])
                nc.sync.dma_start(out=out[:, TILE * (i + 1) - width : TILE * (i + 1)], in_=score[:, 0:width])

        pipeline = (
            (turn, 0),
            (total, 5),
            (classes_v, 3),
            (project, 1),
            (classes_w, 3),
            (gather, 0),
            (store, 5),
            (squash_a, 3),
            (squash_b, 3),
            (regroup, 1),
            (scale_w, 3),
            (quantise_xp, 2),
            (quantise_x, 0),
            (widen, -2),
            (weigh_a, 3),
            (weigh_b, 3),
        )
        once = {-2: reorder_z, 0: path_probabilities}
        lags = [lag for stage, lag in pipeline]
        for s in range(min(lags), TILES + max(lags)):
            for stage, lag in pipeline:
                if 0 <= s - lag < TILES:
                    stage(s - lag)
            if s in once:
                once[s]()
